import numpy as np
import ml_dtypes


def mxq(x, axis, fmt="e4m3"):
    dtype, down = {"e4m3": (ml_dtypes.float8_e4m3fn, 7), "e5m2": (ml_dtypes.float8_e5m2, 14)}[fmt]
    v = np.moveaxis(np.asarray(x, np.float32).astype(ml_dtypes.bfloat16).astype(np.float64), axis, -1)
    blocks = v.reshape(v.shape[:-1] + (-1, 32))
    amax = np.abs(blocks).max(-1, keepdims=True)
    byte = np.maximum(np.where(amax > 0, np.frexp(amax)[1] - 1 + 127, 0) - down, 1)
    scale = np.exp2(byte - 127.0)
    codes = (blocks / scale).astype(np.float32).astype(dtype).astype(np.float64)
    return np.moveaxis((codes * scale).reshape(v.shape), -1, axis)


WIDE = False


def mx_kscale(k):
    if not WIDE:
        return np.ones(k)
    levels = np.array([10, -10, 5, -5, 0])
    if k % 512:
        return np.exp2(np.random.permutation(np.resize(levels, k // 32))).repeat(32)
    a = np.empty((k // 512, 16))
    for p in range(k // 512):
        a[p, :8] = np.random.permutation(np.resize(levels, 8))
        for g in range(8):
            far = levels[np.abs(levels - a[p, g]) >= 10]
            a[p, g + 8] = far[np.random.randint(len(far))]
    return np.exp2(a.ravel()).repeat(32)


BF16 = ml_dtypes.bfloat16


def bf(x):
    return np.asarray(x, np.float32).astype(BF16)


def f64(x):
    return np.asarray(x).astype(np.float64)


B, T, HIDDEN, NUM_HEADS, HEAD_DIM, ROT_DIM, LATENT = 2, 64, 1024, 16, 128, 64, 512
NOPE_DIM = HEAD_DIM - ROT_DIM
BASE = 10000.0


def rope_tables():
    inv_freq = 1.0 / (BASE ** (np.arange(0, ROT_DIM, 2) / ROT_DIM))
    freqs = np.arange(T)[:, None] * inv_freq[None, :]
    emb = np.concatenate((freqs, freqs), axis=-1)
    return np.cos(emb), np.sin(emb)


def rotate_half(v):
    v1, v2 = v[..., : v.shape[-1] // 2], v[..., v.shape[-1] // 2 :]
    return np.concatenate((-v2, v1), axis=-1)


def heads(y, d):
    return y.reshape(B, T, NUM_HEADS, d).transpose(0, 2, 1, 3)


def setup_inputs():
    s, t = mx_kscale(HIDDEN), mx_kscale(LATENT)
    cos, sin = rope_tables()
    return {"x": bf(np.random.standard_normal((B, T, HIDDEN)) * s),
            "Wq_d": bf(np.random.standard_normal((HIDDEN, LATENT)) / np.sqrt(HIDDEN) / s[:, None] * t),
            "Wq_nope": bf(np.random.standard_normal((LATENT, NUM_HEADS * NOPE_DIM)) / np.sqrt(LATENT) / t[:, None]),
            "Wrq": bf(np.random.standard_normal((LATENT, NUM_HEADS * ROT_DIM)) / np.sqrt(LATENT) / t[:, None]),
            "cos": bf(cos), "sin": bf(sin)}


def reference(x, Wq_d, Wq_nope, Wrq, cos, sin):
    q_latent = mxq(f64(x), 2, "e4m3") @ mxq(f64(Wq_d), 0, "e4m3")
    lq = mxq(q_latent, 2, "e4m3")
    q_nope = heads(lq @ mxq(f64(Wq_nope), 0, "e4m3"), NOPE_DIM)
    q_rot = heads(lq @ mxq(f64(Wrq), 0, "e4m3"), ROT_DIM)
    c, sn = f64(cos)[None, None, :, :], f64(sin)[None, None, :, :]
    q_rot = q_rot * c + rotate_half(q_rot) * sn
    return np.concatenate([q_rot, q_nope], axis=-1)

@@ -1,0 +1,234 @@
+from contextlib import ExitStack
+
+import concourse.mybir as mybir
+from concourse.masks import make_identity
+
+BF16 = mybir.dt.bfloat16
+F32 = mybir.dt.float32
+U32 = mybir.dt.uint32
+U8 = mybir.dt.uint8
+FP8X4 = mybir.dt.float8_e4m3fn_x4
+MULT = mybir.AluOpType.mult
+ADD = mybir.AluOpType.add
+SUBTRACT = mybir.AluOpType.subtract
+
+P = 128
+PACK = 4
+K_PASS = P * PACK
+
+BATCH, SEQ, HIDDEN, LATENT = 2, 64, 1024, 512
+HEADS, ROT, NOPE = 16, 64, 64
+HALF_ROT = ROT // 2
+HEAD = ROT + NOPE
+UP = HEADS * ROT
+DOWN_PASSES = HIDDEN // K_PASS
+
+UNIT = 512
+PIECE = UNIT // 2
+FIRST, SECOND = slice(0, PIECE), slice(PIECE, UNIT)
+UNIT_HEADS = UNIT // ROT
+PIECE_HEADS = PIECE // ROT
+NOPE_PIECES = UP // PIECE
+RUN = 4
+EVACUATE_BEHIND = 2
+
+FLOPS = 2 * BATCH * SEQ * (HIDDEN * LATENT + LATENT * 2 * UP)
+
+
+def regroup(copy, weight, cols):
+    copy(
+        out=weight["grouped"][:, cols, :].rearrange("p (c i) j -> p c j i", i=RUN),
+        in_=weight["raw"][:, :, cols].rearrange("p j (c i) -> p c j i", i=RUN),
+    )
+
+
+def regroup_permuted(copy, weight, cols):
+    blocks = slice(cols.start // P, cols.stop // P)
+    copy(
+        out=weight["grouped"][:, cols, :].rearrange("p (t m) j -> p t m j", m=P),
+        in_=weight["raw"][:].rearrange("p j (m t) -> p t m j", t=PACK)[:, blocks],
+    )
+
+
+def quantise(nc, weight, cols):
+    nc.vector.quantize_mx(
+        out=weight["codes"][:, cols].bitcast(FP8X4),
+        scales=weight["scales"][:, cols],
+        in_=weight["grouped"][:, cols, :].rearrange("p c j -> p (c j)"),
+    )
+
+
+def tile_multiheadlatentattention_pa_s_kernel(tc, x, Wq_d, Wq_nope, Wrq, cos, sin, out):
+    nc = tc.nc
+    with ExitStack() as ctx:
+        keep = ctx.enter_context(tc.tile_pool(name="keep", bufs=1))
+        psum = ctx.enter_context(tc.psum_pool(name="psum", bufs=1))
+        ctx.enter_context(tc.manual_schedule())
+
+        def load_weight(name, rows_by_partition):
+            raw = keep.tile([P, PACK, UNIT], BF16, name=name + "_raw")
+            nc.sync.dma_start(out=raw[:], in_=rows_by_partition)
+            return {
+                "raw": raw,
+                "grouped": keep.tile([P, UNIT, PACK], BF16, name=name + "_grouped", align_bytes=64),
+                "codes": keep.tile([P, UNIT], U32, name=name + "_codes", align_bytes=64),
+                "scales": keep.tile([P, UNIT], U8, name=name + "_scales", align_bytes=64),
+            }
+
+        x_sb = keep.tile([P, HIDDEN], BF16)
+        for b in range(BATCH):
+            nc.sync.dma_start(out=x_sb[b:P:BATCH, :], in_=x[b])
+        down = []
+        for g in range(DOWN_PASSES):
+            rows = Wq_d[g * K_PASS : (g + 1) * K_PASS, :]
+            down.append(load_weight("down%d" % g, rows.rearrange("(p j) c -> p j c", j=PACK)))
+        cos_sb = keep.tile([P, ROT], BF16)
+        sin_swapped = keep.tile([P, ROT], BF16)
+        for b in range(BATCH):
+            nc.scalar.dma_start(out=cos_sb[b:P:BATCH, :], in_=cos)
+            nc.scalar.dma_start(out=sin_swapped[b:P:BATCH, 0:HALF_ROT], in_=sin[:, HALF_ROT:ROT])
+            nc.scalar.dma_start(out=sin_swapped[b:P:BATCH, HALF_ROT:ROT], in_=sin[:, 0:HALF_ROT])
+        rot = []
+        nope = []
+        for name, w, units in (("rot", Wrq, rot), ("nope", Wq_nope, nope)):
+            for c in range(UP // UNIT):
+                cols = w[:, c * UNIT : (c + 1) * UNIT]
+                units.append(load_weight("%s%d" % (name, c), cols.rearrange("(p j) n -> p j n", j=PACK)))
+
+        ident = keep.tile([P, P], F32)
+        make_identity(nc, ident[:])
+
+        x_words = x_sb[:].bitcast(F32)
+        xT_ps = psum.tile([P, DOWN_PASSES, 2, P], F32)
+        words_pass = K_PASS // 2
+        for g in range(DOWN_PASSES):
+            for u in range(2):
+                nc.tensor.transpose(
+                    xT_ps[:, g, u, :],
+                    x_words[:, g * words_pass + u : (g + 1) * words_pass : 2],
+                    ident[:],
+                )
+        x_grouped = keep.tile([P, DOWN_PASSES * P * PACK], BF16, align_bytes=64)
+        nc.scalar.copy(
+            out=x_grouped[:].bitcast(F32).rearrange("p (g m u) -> p g m u", g=DOWN_PASSES, u=2),
+            in_=xT_ps[:].rearrange("p g u m -> p g m u"),
+        )
+        x_codes = keep.tile([P, DOWN_PASSES, P], U32, align_bytes=64)
+        x_scales = keep.tile([P, DOWN_PASSES, P], U8, align_bytes=64)
+
+        regroup_permuted(nc.vector.tensor_copy, down[0], FIRST)
+        regroup_permuted(nc.scalar.copy, down[0], SECOND)
+        nc.vector.quantize_mx(
+            out=x_codes[:].rearrange("p g m -> p (g m)").bitcast(FP8X4),
+            scales=x_scales[:].rearrange("p g m -> p (g m)"),
+            in_=x_grouped[:],
+        )
+        quantise(nc, down[0], FIRST)
+        regroup_permuted(nc.vector.tensor_copy, down[1], FIRST)
+        regroup_permuted(nc.scalar.copy, down[1], SECOND)
+        quantise(nc, down[0], SECOND)
+        quantise(nc, down[1], FIRST)
+        quantise(nc, down[1], SECOND)
+
+        latT_ps = psum.tile([P, PACK, P], F32)
+        for j in range(PACK):
+            block = slice(j * P, (j + 1) * P)
+            for g in range(DOWN_PASSES):
+                nc.tensor.matmul_mx(
+                    out=latT_ps[:, j, :],
+                    lhsT=down[g]["codes"][:, block].bitcast(FP8X4),
+                    lhsT_scale=down[g]["scales"][:, block],
+                    rhs=x_codes[:, g, :].bitcast(FP8X4),
+                    rhs_scale=x_scales[:, g, :],
+                    start=(g == 0),
+                    stop=(g == DOWN_PASSES - 1),
+                )
+        lat_grouped = keep.tile([P, P, PACK], BF16, align_bytes=64)
+        lat_codes = keep.tile([P, P], U32, align_bytes=64)
+        lat_scales = keep.tile([P, P], U8, align_bytes=64)
+
+        def up_product(acc, weight, cols):
+            nc.tensor.matmul_mx(
+                out=acc,
+                lhsT=lat_codes[:].bitcast(FP8X4),
+                lhsT_scale=lat_scales[:],
+                rhs=weight["codes"][:, cols].bitcast(FP8X4),
+                rhs_scale=weight["scales"][:, cols],
+                start=True,
+                stop=True,
+            )
+
+        regroup(nc.vector.tensor_copy, rot[0], FIRST)
+        regroup(nc.scalar.copy, rot[0], SECOND)
+        nc.scalar.copy(out=lat_grouped[:], in_=latT_ps[:].rearrange("p j m -> p m j"))
+        quantise(nc, rot[0], FIRST)
+        regroup(nc.vector.tensor_copy, rot[1], FIRST)
+        regroup(nc.scalar.copy, rot[1], SECOND)
+        quantise(nc, rot[0], SECOND)
+        nc.vector.quantize_mx(
+            out=lat_codes[:].bitcast(FP8X4),
+            scales=lat_scales[:],
+            in_=lat_grouped[:].rearrange("p m j -> p (m j)"),
+        )
+        quantise(nc, rot[1], FIRST)
+        quantise(nc, rot[1], SECOND)
+        rot_ps = []
+        for c in range(UP // UNIT):
+            acc = psum.tile([P, UNIT], F32, name="rot_ps%d" % c)
+            for cols in (FIRST, SECOND):
+                up_product(acc[:, cols], rot[c], cols)
+            rot_ps.append(acc)
+
+        out_sb = keep.tile([P, HEADS, HEAD], F32)
+        by_cos = keep.tile([P, HEADS, ROT], F32)
+        by_sin = keep.tile([P, HEADS, ROT], F32)
+        cos_heads = cos_sb[:].unsqueeze(1).to_broadcast([P, UNIT_HEADS, ROT])
+        sin_heads = sin_swapped[:].unsqueeze(1).to_broadcast([P, UNIT_HEADS, ROT])
+
+        def rotation_products(c):
+            heads = slice(c * UNIT_HEADS, (c + 1) * UNIT_HEADS)
+            u = rot_ps[c][:].rearrange("p (h d) -> p h d", d=ROT)
+            nc.vector.tensor_tensor(out=by_cos[:, heads, :], in0=u, in1=cos_heads, op=MULT)
+            nc.vector.tensor_tensor(out=by_sin[:, heads, :], in0=u, in1=sin_heads, op=MULT)
+
+        def rotation_sums(c):
+            heads = slice(c * UNIT_HEADS, (c + 1) * UNIT_HEADS)
+            nc.vector.tensor_tensor(
+                out=out_sb[:, heads, 0:HALF_ROT],
+                in0=by_cos[:, heads, 0:HALF_ROT],
+                in1=by_sin[:, heads, HALF_ROT:ROT],
+                op=SUBTRACT,
+            )
+            nc.vector.tensor_tensor(
+                out=out_sb[:, heads, HALF_ROT:ROT],
+                in0=by_cos[:, heads, HALF_ROT:ROT],
+                in1=by_sin[:, heads, 0:HALF_ROT],
+                op=ADD,
+            )
+
+        nope_ps = []
+        for k in range(NOPE_PIECES + EVACUATE_BEHIND):
+            if k < NOPE_PIECES:
+                c, second = divmod(k, 2)
+                cols = SECOND if second else FIRST
+                regroup(nc.scalar.copy, nope[c], cols)
+                if second:
+                    rotation_sums(c)
+                else:
+                    rotation_products(c)
+                quantise(nc, nope[c], cols)
+                acc = psum.tile([P, PIECE], F32, name="nope_ps%d" % k)
+                up_product(acc[:], nope[c], cols)
+                nope_ps.append(acc)
+            if k >= EVACUATE_BEHIND:
+                done = k - EVACUATE_BEHIND
+                heads = slice(done * PIECE_HEADS, (done + 1) * PIECE_HEADS)
+                nc.scalar.copy(
+                    out=out_sb[:, heads, ROT:HEAD],
+                    in_=nope_ps[done][:].rearrange("p (h d) -> p h d", d=NOPE),
+                )
+                for b in range(BATCH):
+                    nc.sync.dma_start(
+                        out=out[b, heads].rearrange("h t d -> t h d"),
+                        in_=out_sb[b:P:BATCH, heads, :],
+                    )

@@ -42,14 +42,6 @@ def regroup(copy, weight, cols):
     )
 
 
-def regroup_permuted(copy, weight, cols):
-    blocks = slice(cols.start // P, cols.stop // P)
-    copy(
-        out=weight["grouped"][:, cols, :].rearrange("p (t m) j -> p t m j", m=P),
-        in_=weight["raw"][:].rearrange("p j (m t) -> p t m j", t=PACK)[:, blocks],
-    )
-
-
 def quantise(nc, weight, cols):
     nc.vector.quantize_mx(
         out=weight["codes"][:, cols].bitcast(FP8X4),
@@ -64,6 +56,10 @@ def tile_multiheadlatentattention_pa_s_kernel(tc, x, Wq_d, Wq_nope, Wrq, cos, si
         keep = ctx.enter_context(tc.tile_pool(name="keep", bufs=1))
         psum = ctx.enter_context(tc.psum_pool(name="psum", bufs=1))
         ctx.enter_context(tc.manual_schedule())
+
+        warm = keep.tile([P, 2], F32)
+        nc.vector.memset(warm[:], 0.0)
+        nc.scalar.copy(out=warm[:, 1:2], in_=warm[:, 0:1])
 
         def load_weight(name, rows_by_partition):
             raw = keep.tile([P, PACK, UNIT], BF16, name=name + "_raw")
@@ -84,16 +80,17 @@ def tile_multiheadlatentattention_pa_s_kernel(tc, x, Wq_d, Wq_nope, Wrq, cos, si
             down.append(load_weight("down%d" % g, rows.rearrange("(p j) c -> p j c", j=PACK)))
         cos_sb = keep.tile([P, ROT], BF16)
         sin_swapped = keep.tile([P, ROT], BF16)
-        for b in range(BATCH):
-            nc.scalar.dma_start(out=cos_sb[b:P:BATCH, :], in_=cos)
-            nc.scalar.dma_start(out=sin_swapped[b:P:BATCH, 0:HALF_ROT], in_=sin[:, HALF_ROT:ROT])
-            nc.scalar.dma_start(out=sin_swapped[b:P:BATCH, HALF_ROT:ROT], in_=sin[:, 0:HALF_ROT])
         rot = []
         nope = []
         for name, w, units in (("rot", Wrq, rot), ("nope", Wq_nope, nope)):
             for c in range(UP // UNIT):
                 cols = w[:, c * UNIT : (c + 1) * UNIT]
                 units.append(load_weight("%s%d" % (name, c), cols.rearrange("(p j) n -> p j n", j=PACK)))
+            if w is Wrq:
+                for b in range(BATCH):
+                    nc.sync.dma_start(out=cos_sb[b:P:BATCH, :], in_=cos)
+                    nc.sync.dma_start(out=sin_swapped[b:P:BATCH, 0:HALF_ROT], in_=sin[:, HALF_ROT:ROT])
+                    nc.sync.dma_start(out=sin_swapped[b:P:BATCH, HALF_ROT:ROT], in_=sin[:, 0:HALF_ROT])
 
         ident = keep.tile([P, P], F32)
         make_identity(nc, ident[:])
@@ -116,33 +113,33 @@ def tile_multiheadlatentattention_pa_s_kernel(tc, x, Wq_d, Wq_nope, Wrq, cos, si
         x_codes = keep.tile([P, DOWN_PASSES, P], U32, align_bytes=64)
         x_scales = keep.tile([P, DOWN_PASSES, P], U8, align_bytes=64)
 
-        regroup_permuted(nc.vector.tensor_copy, down[0], FIRST)
-        regroup_permuted(nc.scalar.copy, down[0], SECOND)
+        regroup(nc.vector.tensor_copy, down[0], FIRST)
+        regroup(nc.scalar.copy, down[0], SECOND)
         nc.vector.quantize_mx(
             out=x_codes[:].rearrange("p g m -> p (g m)").bitcast(FP8X4),
             scales=x_scales[:].rearrange("p g m -> p (g m)"),
             in_=x_grouped[:],
         )
         quantise(nc, down[0], FIRST)
-        regroup_permuted(nc.vector.tensor_copy, down[1], FIRST)
-        regroup_permuted(nc.scalar.copy, down[1], SECOND)
+        regroup(nc.vector.tensor_copy, down[1], FIRST)
+        regroup(nc.scalar.copy, down[1], SECOND)
         quantise(nc, down[0], SECOND)
         quantise(nc, down[1], FIRST)
         quantise(nc, down[1], SECOND)
 
-        latT_ps = psum.tile([P, PACK, P], F32)
-        for j in range(PACK):
-            block = slice(j * P, (j + 1) * P)
-            for g in range(DOWN_PASSES):
-                nc.tensor.matmul_mx(
-                    out=latT_ps[:, j, :],
-                    lhsT=down[g]["codes"][:, block].bitcast(FP8X4),
-                    lhsT_scale=down[g]["scales"][:, block],
-                    rhs=x_codes[:, g, :].bitcast(FP8X4),
-                    rhs_scale=x_scales[:, g, :],
-                    start=(g == 0),
-                    stop=(g == DOWN_PASSES - 1),
-                )
+        lat_ps = psum.tile([P, LATENT], F32)
+        for g in range(DOWN_PASSES):
+            nc.tensor.matmul_mx(
+                out=lat_ps[:],
+                lhsT=x_codes[:, g, :].bitcast(FP8X4),
+                lhsT_scale=x_scales[:, g, :],
+                rhs=down[g]["codes"][:].bitcast(FP8X4),
+                rhs_scale=down[g]["scales"][:],
+                start=(g == 0),
+                stop=(g == DOWN_PASSES - 1),
+            )
+        lat_sb = keep.tile([P, LATENT], BF16)
+        latT_ps = xT_ps[:, 0]
         lat_grouped = keep.tile([P, P, PACK], BF16, align_bytes=64)
         lat_codes = keep.tile([P, P], U32, align_bytes=64)
         lat_scales = keep.tile([P, P], U8, align_bytes=64)
@@ -160,10 +157,16 @@ def tile_multiheadlatentattention_pa_s_kernel(tc, x, Wq_d, Wq_nope, Wrq, cos, si
 
         regroup(nc.vector.tensor_copy, rot[0], FIRST)
         regroup(nc.scalar.copy, rot[0], SECOND)
-        nc.scalar.copy(out=lat_grouped[:], in_=latT_ps[:].rearrange("p j m -> p m j"))
+        nc.scalar.copy(out=lat_sb[:], in_=lat_ps[:])
+        for u in range(2):
+            nc.tensor.transpose(latT_ps[:, u, :], lat_sb[:].bitcast(F32)[:, u::2], ident[:])
         quantise(nc, rot[0], FIRST)
         regroup(nc.vector.tensor_copy, rot[1], FIRST)
         regroup(nc.scalar.copy, rot[1], SECOND)
+        nc.scalar.copy(
+            out=lat_grouped[:].rearrange("p m j -> p (m j)").bitcast(F32).rearrange("p (m u) -> p m u", u=2),
+            in_=latT_ps.rearrange("p u m -> p m u"),
+        )
         quantise(nc, rot[0], SECOND)
         nc.vector.quantize_mx(
             out=lat_codes[:].bitcast(FP8X4),

@@ -10,7 +10,6 @@ U8 = mybir.dt.uint8
 FP8X4 = mybir.dt.float8_e4m3fn_x4
 MULT = mybir.AluOpType.mult
 ADD = mybir.AluOpType.add
-SUBTRACT = mybir.AluOpType.subtract
 
 P = 128
 PACK = 4
@@ -25,12 +24,11 @@ DOWN_PASSES = HIDDEN // K_PASS
 
 UNIT = 512
 PIECE = UNIT // 2
-FIRST, SECOND = slice(0, PIECE), slice(PIECE, UNIT)
+WHOLE, FIRST, SECOND = slice(0, UNIT), slice(0, PIECE), slice(PIECE, UNIT)
+UNITS = UP // UNIT
 UNIT_HEADS = UNIT // ROT
 PIECE_HEADS = PIECE // ROT
-NOPE_PIECES = UP // PIECE
 RUN = 4
-EVACUATE_BEHIND = 2
 
 FLOPS = 2 * BATCH * SEQ * (HIDDEN * LATENT + LATENT * 2 * UP)
 
@@ -39,6 +37,13 @@ def regroup(copy, weight, cols):
     copy(
         out=weight["grouped"][:, cols, :].rearrange("p (c i) j -> p c j i", i=RUN),
         in_=weight["raw"][:, :, cols].rearrange("p j (c i) -> p c j i", i=RUN),
+    )
+
+
+def regroup_down(copy, weight, groups):
+    copy(
+        out=weight["grouped"][:].rearrange("p (t m) j -> p m t j", t=PACK)[:, groups],
+        in_=weight["raw"][:].rearrange("p j (m t) -> p m t j", t=PACK)[:, groups],
     )
 
 
@@ -72,28 +77,32 @@ def tile_multiheadlatentattention_pa_s_kernel(tc, x, Wq_d, Wq_nope, Wrq, cos, si
             }
 
         x_sb = keep.tile([P, HIDDEN], BF16)
-        for b in range(BATCH):
-            nc.sync.dma_start(out=x_sb[b:P:BATCH, :], in_=x[b])
         down = []
         for g in range(DOWN_PASSES):
             rows = Wq_d[g * K_PASS : (g + 1) * K_PASS, :]
             down.append(load_weight("down%d" % g, rows.rearrange("(p j) c -> p j c", j=PACK)))
-        cos_sb = keep.tile([P, ROT], BF16)
-        sin_swapped = keep.tile([P, ROT], BF16)
+            if g == 0:
+                for b in range(BATCH):
+                    nc.sync.dma_start(out=x_sb[b:P:BATCH, :], in_=x[b])
+        tables = keep.tile([P, 2, ROT], BF16, align_bytes=64)
+        sin_sb = keep.tile([P, ROT], BF16, align_bytes=64)
         rot = []
         nope = []
         for name, w, units in (("rot", Wrq, rot), ("nope", Wq_nope, nope)):
-            for c in range(UP // UNIT):
+            for c in range(UNITS):
                 cols = w[:, c * UNIT : (c + 1) * UNIT]
                 units.append(load_weight("%s%d" % (name, c), cols.rearrange("(p j) n -> p j n", j=PACK)))
             if w is Wrq:
                 for b in range(BATCH):
-                    nc.sync.dma_start(out=cos_sb[b:P:BATCH, :], in_=cos)
-                    nc.sync.dma_start(out=sin_swapped[b:P:BATCH, 0:HALF_ROT], in_=sin[:, HALF_ROT:ROT])
-                    nc.sync.dma_start(out=sin_swapped[b:P:BATCH, HALF_ROT:ROT], in_=sin[:, 0:HALF_ROT])
+                    nc.sync.dma_start(out=tables[b:P:BATCH, 0, :], in_=cos)
+                    nc.sync.dma_start(out=sin_sb[b:P:BATCH, :], in_=sin)
 
         ident = keep.tile([P, P], F32)
         make_identity(nc, ident[:])
+        nc.gpsimd.tensor_copy(out=tables[:, 1, 0:HALF_ROT], in_=sin_sb[:, HALF_ROT:ROT])
+        nc.gpsimd.tensor_scalar(
+            out=tables[:, 1, HALF_ROT:ROT], in0=sin_sb[:, 0:HALF_ROT], scalar1=-1.0, scalar2=None, op0=MULT
+        )
 
         x_words = x_sb[:].bitcast(F32)
         xT_ps = psum.tile([P, DOWN_PASSES, 2, P], F32)
@@ -106,132 +115,132 @@ def tile_multiheadlatentattention_pa_s_kernel(tc, x, Wq_d, Wq_nope, Wrq, cos, si
                     ident[:],
                 )
         x_grouped = keep.tile([P, DOWN_PASSES * P * PACK], BF16, align_bytes=64)
+        x_codes = keep.tile([P, DOWN_PASSES, P], U32, align_bytes=64)
+        x_scales = keep.tile([P, DOWN_PASSES, P], U8, align_bytes=64)
+
+        def regroup_halves(weight, how, first, second):
+            how(nc.vector.tensor_copy, weight, first)
+            how(nc.scalar.copy, weight, second)
+
+        low, high = slice(0, P // 2), slice(P // 2, P)
+        regroup_halves(down[0], regroup_down, low, high)
         nc.scalar.copy(
             out=x_grouped[:].bitcast(F32).rearrange("p (g m u) -> p g m u", g=DOWN_PASSES, u=2),
             in_=xT_ps[:].rearrange("p g u m -> p g m u"),
         )
-        x_codes = keep.tile([P, DOWN_PASSES, P], U32, align_bytes=64)
-        x_scales = keep.tile([P, DOWN_PASSES, P], U8, align_bytes=64)
-
-        regroup(nc.vector.tensor_copy, down[0], FIRST)
-        regroup(nc.scalar.copy, down[0], SECOND)
+        quantise(nc, down[0], WHOLE)
+        regroup_halves(down[1], regroup_down, low, high)
         nc.vector.quantize_mx(
             out=x_codes[:].rearrange("p g m -> p (g m)").bitcast(FP8X4),
             scales=x_scales[:].rearrange("p g m -> p (g m)"),
             in_=x_grouped[:],
         )
-        quantise(nc, down[0], FIRST)
-        regroup(nc.vector.tensor_copy, down[1], FIRST)
-        regroup(nc.scalar.copy, down[1], SECOND)
-        quantise(nc, down[0], SECOND)
-        quantise(nc, down[1], FIRST)
-        quantise(nc, down[1], SECOND)
+        quantise(nc, down[1], WHOLE)
 
-        lat_ps = psum.tile([P, LATENT], F32)
-        for g in range(DOWN_PASSES):
-            nc.tensor.matmul_mx(
-                out=lat_ps[:],
-                lhsT=x_codes[:, g, :].bitcast(FP8X4),
-                lhsT_scale=x_scales[:, g, :],
-                rhs=down[g]["codes"][:].bitcast(FP8X4),
-                rhs_scale=down[g]["scales"][:],
-                start=(g == 0),
-                stop=(g == DOWN_PASSES - 1),
-            )
-        lat_sb = keep.tile([P, LATENT], BF16)
-        latT_ps = xT_ps[:, 0]
+        latT_ps = psum.tile([P, PACK, P], F32)
+        for j in range(PACK):
+            block = slice(j * P, (j + 1) * P)
+            for g in range(DOWN_PASSES):
+                nc.tensor.matmul_mx(
+                    out=latT_ps[:, j, :],
+                    lhsT=down[g]["codes"][:, block].bitcast(FP8X4),
+                    lhsT_scale=down[g]["scales"][:, block],
+                    rhs=x_codes[:, g, :].bitcast(FP8X4),
+                    rhs_scale=x_scales[:, g, :],
+                    start=(g == 0),
+                    stop=(g == DOWN_PASSES - 1),
+                )
         lat_grouped = keep.tile([P, P, PACK], BF16, align_bytes=64)
         lat_codes = keep.tile([P, P], U32, align_bytes=64)
         lat_scales = keep.tile([P, P], U8, align_bytes=64)
 
-        def up_product(acc, weight, cols):
+        def up_product(acc, weight):
             nc.tensor.matmul_mx(
                 out=acc,
                 lhsT=lat_codes[:].bitcast(FP8X4),
                 lhsT_scale=lat_scales[:],
-                rhs=weight["codes"][:, cols].bitcast(FP8X4),
-                rhs_scale=weight["scales"][:, cols],
+                rhs=weight["codes"][:].bitcast(FP8X4),
+                rhs_scale=weight["scales"][:],
                 start=True,
                 stop=True,
             )
 
-        regroup(nc.vector.tensor_copy, rot[0], FIRST)
-        regroup(nc.scalar.copy, rot[0], SECOND)
-        nc.scalar.copy(out=lat_sb[:], in_=lat_ps[:])
-        for u in range(2):
-            nc.tensor.transpose(latT_ps[:, u, :], lat_sb[:].bitcast(F32)[:, u::2], ident[:])
-        quantise(nc, rot[0], FIRST)
-        regroup(nc.vector.tensor_copy, rot[1], FIRST)
-        regroup(nc.scalar.copy, rot[1], SECOND)
-        nc.scalar.copy(
-            out=lat_grouped[:].rearrange("p m j -> p (m j)").bitcast(F32).rearrange("p (m u) -> p m u", u=2),
-            in_=latT_ps.rearrange("p u m -> p m u"),
-        )
-        quantise(nc, rot[0], SECOND)
+        regroup_halves(rot[0], regroup, FIRST, SECOND)
+        regroup_halves(rot[1], regroup, FIRST, SECOND)
+        quantise(nc, rot[0], WHOLE)
+        nc.scalar.copy(out=lat_grouped[:], in_=latT_ps[:].rearrange("p j m -> p m j"))
+        regroup_halves(nope[0], regroup, FIRST, SECOND)
+        quantise(nc, rot[1], WHOLE)
         nc.vector.quantize_mx(
             out=lat_codes[:].bitcast(FP8X4),
             scales=lat_scales[:],
             in_=lat_grouped[:].rearrange("p m j -> p (m j)"),
         )
-        quantise(nc, rot[1], FIRST)
-        quantise(nc, rot[1], SECOND)
+        regroup_halves(nope[1], regroup, FIRST, SECOND)
+        quantise(nc, nope[0], WHOLE)
         rot_ps = []
-        for c in range(UP // UNIT):
-            acc = psum.tile([P, UNIT], F32, name="rot_ps%d" % c)
-            for cols in (FIRST, SECOND):
-                up_product(acc[:, cols], rot[c], cols)
-            rot_ps.append(acc)
+        nope_ps = []
+
+        def product(accs, name, weight):
+            acc = psum.tile([P, UNIT], F32, name=name)
+            up_product(acc[:], weight)
+            accs.append(acc)
+
+        product(rot_ps, "rot_ps0", rot[0])
+        product(rot_ps, "rot_ps1", rot[1])
+        product(nope_ps, "nope_ps0", nope[0])
 
         out_sb = keep.tile([P, HEADS, HEAD], F32)
-        by_cos = keep.tile([P, HEADS, ROT], F32)
-        by_sin = keep.tile([P, HEADS, ROT], F32)
-        cos_heads = cos_sb[:].unsqueeze(1).to_broadcast([P, UNIT_HEADS, ROT])
-        sin_heads = sin_swapped[:].unsqueeze(1).to_broadcast([P, UNIT_HEADS, ROT])
+        products = keep.tile([P, 2, HEADS, ROT], F32)
 
-        def rotation_products(c):
-            heads = slice(c * UNIT_HEADS, (c + 1) * UNIT_HEADS)
-            u = rot_ps[c][:].rearrange("p (h d) -> p h d", d=ROT)
-            nc.vector.tensor_tensor(out=by_cos[:, heads, :], in0=u, in1=cos_heads, op=MULT)
-            nc.vector.tensor_tensor(out=by_sin[:, heads, :], in0=u, in1=sin_heads, op=MULT)
-
-        def rotation_sums(c):
-            heads = slice(c * UNIT_HEADS, (c + 1) * UNIT_HEADS)
+        def rotate(first_head, heads):
+            c, at = divmod(first_head, UNIT_HEADS)
+            span = slice(first_head, first_head + heads)
+            u = rot_ps[c][:].rearrange("p (h d) -> p h d", d=ROT)[:, at : at + heads, :]
             nc.vector.tensor_tensor(
-                out=out_sb[:, heads, 0:HALF_ROT],
-                in0=by_cos[:, heads, 0:HALF_ROT],
-                in1=by_sin[:, heads, HALF_ROT:ROT],
-                op=SUBTRACT,
+                out=products[:, :, span, :],
+                in0=u.unsqueeze(1).to_broadcast([P, 2, heads, ROT]),
+                in1=tables[:].unsqueeze(2).to_broadcast([P, 2, heads, ROT]),
+                op=MULT,
             )
-            nc.vector.tensor_tensor(
-                out=out_sb[:, heads, HALF_ROT:ROT],
-                in0=by_cos[:, heads, HALF_ROT:ROT],
-                in1=by_sin[:, heads, 0:HALF_ROT],
+
+        def add_halves(engine, first_head, heads):
+            span = slice(first_head, first_head + heads)
+            halves = lambda ap: ap.rearrange("p h (s i) -> p h s i", s=2)
+            engine.tensor_tensor(
+                out=halves(out_sb[:, span, 0:ROT]),
+                in0=halves(products[:, 0, span, :]),
+                in1=halves(products[:, 1, span, :])[:, :, ::-1, :],
                 op=ADD,
             )
 
-        nope_ps = []
-        for k in range(NOPE_PIECES + EVACUATE_BEHIND):
-            if k < NOPE_PIECES:
-                c, second = divmod(k, 2)
-                cols = SECOND if second else FIRST
-                regroup(nc.scalar.copy, nope[c], cols)
-                if second:
-                    rotation_sums(c)
-                else:
-                    rotation_products(c)
-                quantise(nc, nope[c], cols)
-                acc = psum.tile([P, PIECE], F32, name="nope_ps%d" % k)
-                up_product(acc[:], nope[c], cols)
-                nope_ps.append(acc)
-            if k >= EVACUATE_BEHIND:
-                done = k - EVACUATE_BEHIND
-                heads = slice(done * PIECE_HEADS, (done + 1) * PIECE_HEADS)
-                nc.scalar.copy(
-                    out=out_sb[:, heads, ROT:HEAD],
-                    in_=nope_ps[done][:].rearrange("p (h d) -> p h d", d=NOPE),
+        def evacuate_nope(c):
+            nc.scalar.copy(
+                out=out_sb[:, c * UNIT_HEADS : (c + 1) * UNIT_HEADS, ROT:HEAD],
+                in_=nope_ps[c][:].rearrange("p (h d) -> p h d", d=NOPE),
+            )
+
+        def store(first_head, heads):
+            span = slice(first_head, first_head + heads)
+            for b in range(BATCH):
+                nc.sync.dma_start(
+                    out=out[b, span].rearrange("h t d -> t h d"),
+                    in_=out_sb[b:P:BATCH, span, :],
                 )
-                for b in range(BATCH):
-                    nc.sync.dma_start(
-                        out=out[b, heads].rearrange("h t d -> t h d"),
-                        in_=out_sb[b:P:BATCH, heads, :],
-                    )
+
+        first_unit = range(0, UNIT_HEADS, PIECE_HEADS)
+        second_unit = range(UNIT_HEADS, HEADS, PIECE_HEADS)
+        for first_head in first_unit:
+            rotate(first_head, PIECE_HEADS)
+        evacuate_nope(0)
+        for first_head in first_unit:
+            add_halves(nc.gpsimd, first_head, PIECE_HEADS)
+            store(first_head, PIECE_HEADS)
+        quantise(nc, nope[1], WHOLE)
+        product(nope_ps, "nope_ps1", nope[1])
+        for first_head in second_unit:
+            rotate(first_head, PIECE_HEADS)
+        evacuate_nope(1)
+        for first_head in second_unit:
+            add_halves(nc.vector, first_head, PIECE_HEADS)
+            store(first_head, PIECE_HEADS)

@@ -43,7 +43,7 @@ def regroup(copy, weight, cols):
 def regroup_down(copy, weight, groups):
     copy(
         out=weight["grouped"][:].rearrange("p (t m) j -> p m t j", t=PACK)[:, groups],
-        in_=weight["raw"][:].rearrange("p j (m t) -> p m t j", t=PACK)[:, groups],
+        in_=weight["raw"].rearrange("p j (m t) -> p m t j", t=PACK)[:, groups],
     )
 
 
@@ -66,36 +66,35 @@ def tile_multiheadlatentattention_pa_s_kernel(tc, x, Wq_d, Wq_nope, Wrq, cos, si
         nc.vector.memset(warm[:], 0.0)
         nc.scalar.copy(out=warm[:, 1:2], in_=warm[:, 0:1])
 
-        def load_weight(name, rows_by_partition):
-            raw = keep.tile([P, PACK, UNIT], BF16, name=name + "_raw")
-            nc.sync.dma_start(out=raw[:], in_=rows_by_partition)
-            return {
-                "raw": raw,
-                "grouped": keep.tile([P, UNIT, PACK], BF16, name=name + "_grouped", align_bytes=64),
-                "codes": keep.tile([P, UNIT], U32, name=name + "_codes", align_bytes=64),
-                "scales": keep.tile([P, UNIT], U8, name=name + "_scales", align_bytes=64),
-            }
+        def load_weight(name, rows):
+            width = rows.shape[1]
+            raw = keep.tile([P, PACK, width], BF16, name=name + "_raw")
+            nc.sync.dma_start(out=raw[:], in_=rows.rearrange("(p j) c -> p j c", j=PACK))
+            units = []
+            for c in range(width // UNIT):
+                unit = "%s%d_" % (name, c)
+                units.append({
+                    "raw": raw[:, :, c * UNIT : (c + 1) * UNIT],
+                    "grouped": keep.tile([P, UNIT, PACK], BF16, name=unit + "grouped", align_bytes=64),
+                    "codes": keep.tile([P, UNIT], U32, name=unit + "codes", align_bytes=64),
+                    "scales": keep.tile([P, UNIT], U8, name=unit + "scales", align_bytes=64),
+                })
+            return units
 
         x_sb = keep.tile([P, HIDDEN], BF16)
         down = []
         for g in range(DOWN_PASSES):
-            rows = Wq_d[g * K_PASS : (g + 1) * K_PASS, :]
-            down.append(load_weight("down%d" % g, rows.rearrange("(p j) c -> p j c", j=PACK)))
+            down += load_weight("down%d" % g, Wq_d[g * K_PASS : (g + 1) * K_PASS, :])
             if g == 0:
                 for b in range(BATCH):
                     nc.sync.dma_start(out=x_sb[b:P:BATCH, :], in_=x[b])
         tables = keep.tile([P, 2, ROT], BF16, align_bytes=64)
         sin_sb = keep.tile([P, ROT], BF16, align_bytes=64)
-        rot = []
-        nope = []
-        for name, w, units in (("rot", Wrq, rot), ("nope", Wq_nope, nope)):
-            for c in range(UNITS):
-                cols = w[:, c * UNIT : (c + 1) * UNIT]
-                units.append(load_weight("%s%d" % (name, c), cols.rearrange("(p j) n -> p j n", j=PACK)))
-            if w is Wrq:
-                for b in range(BATCH):
-                    nc.sync.dma_start(out=tables[b:P:BATCH, 0, :], in_=cos)
-                    nc.sync.dma_start(out=sin_sb[b:P:BATCH, :], in_=sin)
+        rot = load_weight("rot", Wrq)
+        for b in range(BATCH):
+            nc.sync.dma_start(out=tables[b:P:BATCH, 0, :], in_=cos)
+            nc.sync.dma_start(out=sin_sb[b:P:BATCH, :], in_=sin)
+        nope = load_weight("nope", Wq_nope)
 
         ident = keep.tile([P, P], F32)
         make_identity(nc, ident[:])

@@ -67,34 +67,34 @@ def tile_multiheadlatentattention_pa_s_kernel(tc, x, Wq_d, Wq_nope, Wrq, cos, si
         nc.scalar.copy(out=warm[:, 1:2], in_=warm[:, 0:1])
 
         def load_weight(name, rows):
-            width = rows.shape[1]
-            raw = keep.tile([P, PACK, width], BF16, name=name + "_raw")
+            raw = keep.tile([P, PACK, UNIT], BF16, name=name + "_raw")
             nc.sync.dma_start(out=raw[:], in_=rows.rearrange("(p j) c -> p j c", j=PACK))
-            units = []
-            for c in range(width // UNIT):
-                unit = "%s%d_" % (name, c)
-                units.append({
-                    "raw": raw[:, :, c * UNIT : (c + 1) * UNIT],
-                    "grouped": keep.tile([P, UNIT, PACK], BF16, name=unit + "grouped", align_bytes=64),
-                    "codes": keep.tile([P, UNIT], U32, name=unit + "codes", align_bytes=64),
-                    "scales": keep.tile([P, UNIT], U8, name=unit + "scales", align_bytes=64),
-                })
-            return units
+            return {
+                "raw": raw[:],
+                "grouped": keep.tile([P, UNIT, PACK], BF16, name=name + "_grouped", align_bytes=64),
+                "codes": keep.tile([P, UNIT], U32, name=name + "_codes", align_bytes=64),
+                "scales": keep.tile([P, UNIT], U8, name=name + "_scales", align_bytes=64),
+            }
 
         x_sb = keep.tile([P, HIDDEN], BF16)
         down = []
         for g in range(DOWN_PASSES):
-            down += load_weight("down%d" % g, Wq_d[g * K_PASS : (g + 1) * K_PASS, :])
+            down.append(load_weight("down%d" % g, Wq_d[g * K_PASS : (g + 1) * K_PASS, :]))
             if g == 0:
                 for b in range(BATCH):
                     nc.sync.dma_start(out=x_sb[b:P:BATCH, :], in_=x[b])
         tables = keep.tile([P, 2, ROT], BF16, align_bytes=64)
         sin_sb = keep.tile([P, ROT], BF16, align_bytes=64)
-        rot = load_weight("rot", Wrq)
-        for b in range(BATCH):
-            nc.sync.dma_start(out=tables[b:P:BATCH, 0, :], in_=cos)
-            nc.sync.dma_start(out=sin_sb[b:P:BATCH, :], in_=sin)
-        nope = load_weight("nope", Wq_nope)
+        rot = []
+        nope = []
+        for c in range(UNITS):
+            cols = slice(c * UNIT, (c + 1) * UNIT)
+            rot.append(load_weight("rot%d" % c, Wrq[:, cols]))
+            nope.append(load_weight("nope%d" % c, Wq_nope[:, cols]))
+            if c == 0:
+                for b in range(BATCH):
+                    nc.sync.dma_start(out=tables[b:P:BATCH, 0, :], in_=cos)
+                    nc.sync.dma_start(out=sin_sb[b:P:BATCH, :], in_=sin)
 
         ident = keep.tile([P, P], F32)
         make_identity(nc, ident[:])
@@ -102,6 +102,17 @@ def tile_multiheadlatentattention_pa_s_kernel(tc, x, Wq_d, Wq_nope, Wrq, cos, si
         nc.gpsimd.tensor_scalar(
             out=tables[:, 1, HALF_ROT:ROT], in0=sin_sb[:, 0:HALF_ROT], scalar1=-1.0, scalar2=None, op0=MULT
         )
+
+        spin_ps = psum.tile([P, P], F32)
+
+        def spin(times, moving):
+            for i in range(times):
+                nc.tensor.matmul(out=spin_ps[:], lhsT=ident[:], rhs=moving, start=True, stop=True)
+
+        def words_of(weight):
+            return weight["raw"][:, 0, 0 : 2 * P].bitcast(F32)
+
+        spin(4, ident[:])
 
         x_words = x_sb[:].bitcast(F32)
         xT_ps = psum.tile([P, DOWN_PASSES, 2, P], F32)
@@ -113,6 +124,7 @@ def tile_multiheadlatentattention_pa_s_kernel(tc, x, Wq_d, Wq_nope, Wrq, cos, si
                     x_words[:, g * words_pass + u : (g + 1) * words_pass : 2],
                     ident[:],
                 )
+        spin(2, words_of(down[1]))
         x_grouped = keep.tile([P, DOWN_PASSES * P * PACK], BF16, align_bytes=64)
         x_codes = keep.tile([P, DOWN_PASSES, P], U32, align_bytes=64)
         x_scales = keep.tile([P, DOWN_PASSES, P], U8, align_bytes=64)
@@ -121,19 +133,19 @@ def tile_multiheadlatentattention_pa_s_kernel(tc, x, Wq_d, Wq_nope, Wrq, cos, si
             how(nc.vector.tensor_copy, weight, first)
             how(nc.scalar.copy, weight, second)
 
-        low, high = slice(0, P // 2), slice(P // 2, P)
-        regroup_halves(down[0], regroup_down, low, high)
+        regroup_halves(down[0], regroup_down, slice(0, 3 * P // 4), slice(3 * P // 4, P))
         nc.scalar.copy(
             out=x_grouped[:].bitcast(F32).rearrange("p (g m u) -> p g m u", g=DOWN_PASSES, u=2),
             in_=xT_ps[:].rearrange("p g u m -> p g m u"),
         )
         quantise(nc, down[0], WHOLE)
-        regroup_halves(down[1], regroup_down, low, high)
+        regroup_halves(down[1], regroup_down, slice(0, P // 2), slice(P // 2, P))
         nc.vector.quantize_mx(
             out=x_codes[:].rearrange("p g m -> p (g m)").bitcast(FP8X4),
             scales=x_scales[:].rearrange("p g m -> p (g m)"),
             in_=x_grouped[:],
         )
+        regroup_halves(rot[0], regroup, FIRST, SECOND)
         quantise(nc, down[1], WHOLE)
 
         latT_ps = psum.tile([P, PACK, P], F32)
@@ -153,6 +165,8 @@ def tile_multiheadlatentattention_pa_s_kernel(tc, x, Wq_d, Wq_nope, Wrq, cos, si
         lat_codes = keep.tile([P, P], U32, align_bytes=64)
         lat_scales = keep.tile([P, P], U8, align_bytes=64)
 
+        spin(3, words_of(rot[1]))
+
         def up_product(acc, weight):
             nc.tensor.matmul_mx(
                 out=acc,
@@ -164,19 +178,19 @@ def tile_multiheadlatentattention_pa_s_kernel(tc, x, Wq_d, Wq_nope, Wrq, cos, si
                 stop=True,
             )
 
-        regroup_halves(rot[0], regroup, FIRST, SECOND)
-        regroup_halves(rot[1], regroup, FIRST, SECOND)
+        regroup_halves(nope[0], regroup, FIRST, SECOND)
         quantise(nc, rot[0], WHOLE)
         nc.scalar.copy(out=lat_grouped[:], in_=latT_ps[:].rearrange("p j m -> p m j"))
-        regroup_halves(nope[0], regroup, FIRST, SECOND)
-        quantise(nc, rot[1], WHOLE)
+        regroup_halves(rot[1], regroup, FIRST, SECOND)
         nc.vector.quantize_mx(
             out=lat_codes[:].bitcast(FP8X4),
             scales=lat_scales[:],
             in_=lat_grouped[:].rearrange("p m j -> p (m j)"),
         )
-        regroup_halves(nope[1], regroup, FIRST, SECOND)
         quantise(nc, nope[0], WHOLE)
+        for cols in (FIRST, SECOND):
+            regroup(nc.scalar.copy, nope[1], cols)
+        quantise(nc, rot[1], WHOLE)
         rot_ps = []
         nope_ps = []
 
@@ -186,8 +200,8 @@ def tile_multiheadlatentattention_pa_s_kernel(tc, x, Wq_d, Wq_nope, Wrq, cos, si
             accs.append(acc)
 
         product(rot_ps, "rot_ps0", rot[0])
-        product(rot_ps, "rot_ps1", rot[1])
         product(nope_ps, "nope_ps0", nope[0])
+        product(rot_ps, "rot_ps1", rot[1])
 
         out_sb = keep.tile([P, HEADS, HEAD], F32)
         products = keep.tile([P, 2, HEADS, ROT], F32)
@@ -203,10 +217,10 @@ def tile_multiheadlatentattention_pa_s_kernel(tc, x, Wq_d, Wq_nope, Wrq, cos, si
                 op=MULT,
             )
 
-        def add_halves(engine, first_head, heads):
+        def add_halves(first_head, heads):
             span = slice(first_head, first_head + heads)
             halves = lambda ap: ap.rearrange("p h (s i) -> p h s i", s=2)
-            engine.tensor_tensor(
+            nc.vector.tensor_tensor(
                 out=halves(out_sb[:, span, 0:ROT]),
                 in0=halves(products[:, 0, span, :]),
                 in1=halves(products[:, 1, span, :])[:, :, ::-1, :],
@@ -232,14 +246,15 @@ def tile_multiheadlatentattention_pa_s_kernel(tc, x, Wq_d, Wq_nope, Wrq, cos, si
         for first_head in first_unit:
             rotate(first_head, PIECE_HEADS)
         evacuate_nope(0)
-        for first_head in first_unit:
-            add_halves(nc.gpsimd, first_head, PIECE_HEADS)
-            store(first_head, PIECE_HEADS)
+        add_halves(0, PIECE_HEADS)
+        store(0, PIECE_HEADS)
         quantise(nc, nope[1], WHOLE)
         product(nope_ps, "nope_ps1", nope[1])
+        add_halves(PIECE_HEADS, PIECE_HEADS)
+        store(PIECE_HEADS, PIECE_HEADS)
         for first_head in second_unit:
             rotate(first_head, PIECE_HEADS)
         evacuate_nope(1)
         for first_head in second_unit:
-            add_halves(nc.vector, first_head, PIECE_HEADS)
+            add_halves(first_head, PIECE_HEADS)
             store(first_head, PIECE_HEADS)

@@ -42,8 +42,8 @@ def regroup(copy, weight, cols):
 
 def regroup_down(copy, weight, groups):
     copy(
-        out=weight["grouped"][:].rearrange("p (t m) j -> p m t j", t=PACK)[:, groups],
-        in_=weight["raw"].rearrange("p j (m t) -> p m t j", t=PACK)[:, groups],
+        out=weight["grouped"][:].rearrange("p (t m) j -> p m j t", t=PACK)[:, groups],
+        in_=weight["raw"].rearrange("p j (m t) -> p m j t", t=PACK)[:, groups],
     )
 
 
@@ -167,13 +167,13 @@ def tile_multiheadlatentattention_pa_s_kernel(tc, x, Wq_d, Wq_nope, Wrq, cos, si
 
         spin(3, words_of(rot[1]))
 
-        def up_product(acc, weight):
+        def up_product(acc, weight, cols):
             nc.tensor.matmul_mx(
                 out=acc,
                 lhsT=lat_codes[:].bitcast(FP8X4),
                 lhsT_scale=lat_scales[:],
-                rhs=weight["codes"][:].bitcast(FP8X4),
-                rhs_scale=weight["scales"][:],
+                rhs=weight["codes"][:, cols].bitcast(FP8X4),
+                rhs_scale=weight["scales"][:, cols],
                 start=True,
                 stop=True,
             )
@@ -188,20 +188,17 @@ def tile_multiheadlatentattention_pa_s_kernel(tc, x, Wq_d, Wq_nope, Wrq, cos, si
             in_=lat_grouped[:].rearrange("p m j -> p (m j)"),
         )
         quantise(nc, nope[0], WHOLE)
-        for cols in (FIRST, SECOND):
-            regroup(nc.scalar.copy, nope[1], cols)
+        regroup(nc.scalar.copy, nope[1], FIRST)
         quantise(nc, rot[1], WHOLE)
-        rot_ps = []
-        nope_ps = []
 
-        def product(accs, name, weight):
+        def product(name, weight, cols=WHOLE):
             acc = psum.tile([P, UNIT], F32, name=name)
-            up_product(acc[:], weight)
-            accs.append(acc)
+            up_product(acc[:, 0 : cols.stop - cols.start], weight, cols)
+            return acc
 
-        product(rot_ps, "rot_ps0", rot[0])
-        product(nope_ps, "nope_ps0", nope[0])
-        product(rot_ps, "rot_ps1", rot[1])
+        rot_ps = [product("rot_ps0", rot[0])]
+        nope0_ps = product("nope0_ps", nope[0])
+        rot_ps.append(product("rot_ps1", rot[1]))
 
         out_sb = keep.tile([P, HEADS, HEAD], F32)
         products = keep.tile([P, 2, HEADS, ROT], F32)
@@ -227,10 +224,10 @@ def tile_multiheadlatentattention_pa_s_kernel(tc, x, Wq_d, Wq_nope, Wrq, cos, si
                 op=ADD,
             )
 
-        def evacuate_nope(c):
+        def evacuate_nope(acc, first_head, heads):
             nc.scalar.copy(
-                out=out_sb[:, c * UNIT_HEADS : (c + 1) * UNIT_HEADS, ROT:HEAD],
-                in_=nope_ps[c][:].rearrange("p (h d) -> p h d", d=NOPE),
+                out=out_sb[:, first_head : first_head + heads, ROT:HEAD],
+                in_=acc[:, 0 : heads * NOPE].rearrange("p (h d) -> p h d", d=NOPE),
             )
 
         def store(first_head, heads):
@@ -242,19 +239,23 @@ def tile_multiheadlatentattention_pa_s_kernel(tc, x, Wq_d, Wq_nope, Wrq, cos, si
                 )
 
         first_unit = range(0, UNIT_HEADS, PIECE_HEADS)
-        second_unit = range(UNIT_HEADS, HEADS, PIECE_HEADS)
         for first_head in first_unit:
             rotate(first_head, PIECE_HEADS)
-        evacuate_nope(0)
-        add_halves(0, PIECE_HEADS)
-        store(0, PIECE_HEADS)
-        quantise(nc, nope[1], WHOLE)
-        product(nope_ps, "nope_ps1", nope[1])
-        add_halves(PIECE_HEADS, PIECE_HEADS)
-        store(PIECE_HEADS, PIECE_HEADS)
-        for first_head in second_unit:
-            rotate(first_head, PIECE_HEADS)
-        evacuate_nope(1)
-        for first_head in second_unit:
+        evacuate_nope(nope0_ps, 0, UNIT_HEADS)
+        for first_head in first_unit:
             add_halves(first_head, PIECE_HEADS)
             store(first_head, PIECE_HEADS)
+        regroup(nc.scalar.copy, nope[1], SECOND)
+        third, last = range(UNIT_HEADS, HEADS, PIECE_HEADS)
+        quantise(nc, nope[1], FIRST)
+        third_ps = product("third_ps", nope[1], FIRST)
+        rotate(third, PIECE_HEADS)
+        quantise(nc, nope[1], SECOND)
+        last_ps = product("last_ps", nope[1], SECOND)
+        evacuate_nope(third_ps, third, PIECE_HEADS)
+        add_halves(third, PIECE_HEADS)
+        store(third, PIECE_HEADS)
+        rotate(last, PIECE_HEADS)
+        evacuate_nope(last_ps, last, PIECE_HEADS)
+        add_halves(last, PIECE_HEADS)
+        store(last, PIECE_HEADS)

@@ -98,10 +98,6 @@ def tile_multiheadlatentattention_pa_s_kernel(tc, x, Wq_d, Wq_nope, Wrq, cos, si
 
         ident = keep.tile([P, P], F32)
         make_identity(nc, ident[:])
-        nc.gpsimd.tensor_copy(out=tables[:, 1, 0:HALF_ROT], in_=sin_sb[:, HALF_ROT:ROT])
-        nc.gpsimd.tensor_scalar(
-            out=tables[:, 1, HALF_ROT:ROT], in0=sin_sb[:, 0:HALF_ROT], scalar1=-1.0, scalar2=None, op0=MULT
-        )
 
         spin_ps = psum.tile([P, P], F32)
 
@@ -133,7 +129,7 @@ def tile_multiheadlatentattention_pa_s_kernel(tc, x, Wq_d, Wq_nope, Wrq, cos, si
             how(nc.vector.tensor_copy, weight, first)
             how(nc.scalar.copy, weight, second)
 
-        regroup_halves(down[0], regroup_down, slice(0, 3 * P // 4), slice(3 * P // 4, P))
+        regroup_halves(down[0], regroup_down, slice(0, 5 * P // 8), slice(5 * P // 8, P))
         nc.scalar.copy(
             out=x_grouped[:].bitcast(F32).rearrange("p (g m u) -> p g m u", g=DOWN_PASSES, u=2),
             in_=xT_ps[:].rearrange("p g u m -> p g m u"),
@@ -181,7 +177,9 @@ def tile_multiheadlatentattention_pa_s_kernel(tc, x, Wq_d, Wq_nope, Wrq, cos, si
         regroup_halves(nope[0], regroup, FIRST, SECOND)
         quantise(nc, rot[0], WHOLE)
         nc.scalar.copy(out=lat_grouped[:], in_=latT_ps[:].rearrange("p j m -> p m j"))
-        regroup_halves(rot[1], regroup, FIRST, SECOND)
+        nc.scalar.copy(out=tables[:, 1, 0:HALF_ROT], in_=sin_sb[:, HALF_ROT:ROT])
+        nc.scalar.mul(tables[:, 1, HALF_ROT:ROT], sin_sb[:, 0:HALF_ROT], -1.0)
+        regroup_halves(rot[1], regroup, slice(0, 5 * UNIT // 8), slice(5 * UNIT // 8, UNIT))
         nc.vector.quantize_mx(
             out=lat_codes[:].bitcast(FP8X4),
             scales=lat_scales[:],
@@ -238,24 +236,32 @@ def tile_multiheadlatentattention_pa_s_kernel(tc, x, Wq_d, Wq_nope, Wrq, cos, si
                     in_=out_sb[b:P:BATCH, span, :],
                 )
 
-        first_unit = range(0, UNIT_HEADS, PIECE_HEADS)
-        for first_head in first_unit:
-            rotate(first_head, PIECE_HEADS)
-        evacuate_nope(nope0_ps, 0, UNIT_HEADS)
-        for first_head in first_unit:
-            add_halves(first_head, PIECE_HEADS)
-            store(first_head, PIECE_HEADS)
-        regroup(nc.scalar.copy, nope[1], SECOND)
-        third, last = range(UNIT_HEADS, HEADS, PIECE_HEADS)
+        first, second, third, last = range(0, HEADS, PIECE_HEADS)
+
+        def halves_of(first_head):
+            return (first_head, first_head + PIECE_HEADS // 2)
+
+        for head in halves_of(first):
+            rotate(head, PIECE_HEADS // 2)
+        evacuate_nope(nope0_ps, first, UNIT_HEADS)
+        for head in halves_of(first):
+            add_halves(head, PIECE_HEADS // 2)
+        store(first, PIECE_HEADS)
+        rotate(second, PIECE_HEADS)
         quantise(nc, nope[1], FIRST)
         third_ps = product("third_ps", nope[1], FIRST)
+        add_halves(second, PIECE_HEADS)
+        store(second, PIECE_HEADS)
+        regroup(nc.scalar.copy, nope[1], SECOND)
         rotate(third, PIECE_HEADS)
         quantise(nc, nope[1], SECOND)
         last_ps = product("last_ps", nope[1], SECOND)
         evacuate_nope(third_ps, third, PIECE_HEADS)
         add_halves(third, PIECE_HEADS)
         store(third, PIECE_HEADS)
-        rotate(last, PIECE_HEADS)
         evacuate_nope(last_ps, last, PIECE_HEADS)
-        add_halves(last, PIECE_HEADS)
-        store(last, PIECE_HEADS)
+        for head in halves_of(last):
+            rotate(head, PIECE_HEADS // 2)
+        for head in halves_of(last):
+            add_halves(head, PIECE_HEADS // 2)
+            store(head, PIECE_HEADS // 2)

from contextlib import ExitStack

import concourse.mybir as mybir
from concourse.masks import make_identity

BF16 = mybir.dt.bfloat16
F32 = mybir.dt.float32
U32 = mybir.dt.uint32
U8 = mybir.dt.uint8
FP8X4 = mybir.dt.float8_e4m3fn_x4
MULT = mybir.AluOpType.mult
ADD = mybir.AluOpType.add

P = 128
PACK = 4
K_PASS = P * PACK

BATCH, SEQ, HIDDEN, LATENT = 2, 64, 1024, 512
HEADS, ROT, NOPE = 16, 64, 64
HALF_ROT = ROT // 2
HEAD = ROT + NOPE
UP = HEADS * ROT
DOWN_PASSES = HIDDEN // K_PASS

UNIT = 512
PIECE = UNIT // 2
WHOLE, FIRST, SECOND = slice(0, UNIT), slice(0, PIECE), slice(PIECE, UNIT)
UNITS = UP // UNIT
UNIT_HEADS = UNIT // ROT
PIECE_HEADS = PIECE // ROT
RUN = 4

FLOPS = 2 * BATCH * SEQ * (HIDDEN * LATENT + LATENT * 2 * UP)


def regroup(copy, weight, cols):
    copy(
        out=weight["grouped"][:, cols, :].rearrange("p (c i) j -> p c j i", i=RUN),
        in_=weight["raw"][:, :, cols].rearrange("p j (c i) -> p c j i", i=RUN),
    )


def regroup_down(copy, weight, groups):
    copy(
        out=weight["grouped"][:].rearrange("p (t m) j -> p m j t", t=PACK)[:, groups],
        in_=weight["raw"].rearrange("p j (m t) -> p m j t", t=PACK)[:, groups],
    )


def quantise(nc, weight, cols):
    nc.vector.quantize_mx(
        out=weight["codes"][:, cols].bitcast(FP8X4),
        scales=weight["scales"][:, cols],
        in_=weight["grouped"][:, cols, :].rearrange("p c j -> p (c j)"),
    )


def tile_multiheadlatentattention_pa_s_kernel(tc, x, Wq_d, Wq_nope, Wrq, cos, sin, out):
    nc = tc.nc
    with ExitStack() as ctx:
        keep = ctx.enter_context(tc.tile_pool(name="keep", bufs=1))
        psum = ctx.enter_context(tc.psum_pool(name="psum", bufs=1))
        ctx.enter_context(tc.manual_schedule())

        warm = keep.tile([P, 2], F32)
        nc.vector.memset(warm[:], 0.0)
        nc.scalar.copy(out=warm[:, 1:2], in_=warm[:, 0:1])

        def load_weight(name, rows):
            raw = keep.tile([P, PACK, UNIT], BF16, name=name + "_raw")
            nc.sync.dma_start(out=raw[:], in_=rows.rearrange("(p j) c -> p j c", j=PACK))
            return {
                "raw": raw[:],
                "grouped": keep.tile([P, UNIT, PACK], BF16, name=name + "_grouped", align_bytes=64),
                "codes": keep.tile([P, UNIT], U32, name=name + "_codes", align_bytes=64),
                "scales": keep.tile([P, UNIT], U8, name=name + "_scales", align_bytes=64),
            }

        x_sb = keep.tile([P, HIDDEN], BF16)
        down = []
        for g in range(DOWN_PASSES):
            down.append(load_weight("down%d" % g, Wq_d[g * K_PASS : (g + 1) * K_PASS, :]))
            if g == 0:
                for b in range(BATCH):
                    nc.sync.dma_start(out=x_sb[b:P:BATCH, :], in_=x[b])
        tables = keep.tile([P, 2, ROT], BF16, align_bytes=64)
        sin_sb = keep.tile([P, ROT], BF16, align_bytes=64)
        rot = []
        nope = []
        for c in range(UNITS):
            cols = slice(c * UNIT, (c + 1) * UNIT)
            rot.append(load_weight("rot%d" % c, Wrq[:, cols]))
            nope.append(load_weight("nope%d" % c, Wq_nope[:, cols]))
            if c == 0:
                for b in range(BATCH):
                    nc.sync.dma_start(out=tables[b:P:BATCH, 0, :], in_=cos)
                    nc.sync.dma_start(out=sin_sb[b:P:BATCH, :], in_=sin)

        ident = keep.tile([P, P], F32)
        make_identity(nc, ident[:])

        spin_ps = psum.tile([P, P], F32)

        def spin(times, moving):
            for i in range(times):
                nc.tensor.matmul(out=spin_ps[:], lhsT=ident[:], rhs=moving, start=True, stop=True)

        def words_of(weight):
            return weight["raw"][:, 0, 0 : 2 * P].bitcast(F32)

        spin(4, ident[:])

        x_words = x_sb[:].bitcast(F32)
        xT_ps = psum.tile([P, DOWN_PASSES, 2, P], F32)
        words_pass = K_PASS // 2
        for g in range(DOWN_PASSES):
            for u in range(2):
                nc.tensor.transpose(
                    xT_ps[:, g, u, :],
                    x_words[:, g * words_pass + u : (g + 1) * words_pass : 2],
                    ident[:],
                )
        spin(2, words_of(down[1]))
        x_grouped = keep.tile([P, DOWN_PASSES * P * PACK], BF16, align_bytes=64)
        x_codes = keep.tile([P, DOWN_PASSES, P], U32, align_bytes=64)
        x_scales = keep.tile([P, DOWN_PASSES, P], U8, align_bytes=64)

        def regroup_halves(weight, how, first, second):
            how(nc.vector.tensor_copy, weight, first)
            how(nc.scalar.copy, weight, second)

        regroup_halves(down[0], regroup_down, slice(0, 5 * P // 8), slice(5 * P // 8, P))
        nc.scalar.copy(
            out=x_grouped[:].bitcast(F32).rearrange("p (g m u) -> p g m u", g=DOWN_PASSES, u=2),
            in_=xT_ps[:].rearrange("p g u m -> p g m u"),
        )
        quantise(nc, down[0], WHOLE)
        regroup_halves(down[1], regroup_down, slice(0, P // 2), slice(P // 2, P))
        nc.vector.quantize_mx(
            out=x_codes[:].rearrange("p g m -> p (g m)").bitcast(FP8X4),
            scales=x_scales[:].rearrange("p g m -> p (g m)"),
            in_=x_grouped[:],
        )
        regroup_halves(rot[0], regroup, FIRST, SECOND)
        quantise(nc, down[1], WHOLE)

        latT_ps = psum.tile([P, PACK, P], F32)
        for j in range(PACK):
            block = slice(j * P, (j + 1) * P)
            for g in range(DOWN_PASSES):
                nc.tensor.matmul_mx(
                    out=latT_ps[:, j, :],
                    lhsT=down[g]["codes"][:, block].bitcast(FP8X4),
                    lhsT_scale=down[g]["scales"][:, block],
                    rhs=x_codes[:, g, :].bitcast(FP8X4),
                    rhs_scale=x_scales[:, g, :],
                    start=(g == 0),
                    stop=(g == DOWN_PASSES - 1),
                )
        lat_grouped = keep.tile([P, P, PACK], BF16, align_bytes=64)
        lat_codes = keep.tile([P, P], U32, align_bytes=64)
        lat_scales = keep.tile([P, P], U8, align_bytes=64)

        spin(3, words_of(rot[1]))

        def up_product(acc, weight, cols):
            nc.tensor.matmul_mx(
                out=acc,
                lhsT=lat_codes[:].bitcast(FP8X4),
                lhsT_scale=lat_scales[:],
                rhs=weight["codes"][:, cols].bitcast(FP8X4),
                rhs_scale=weight["scales"][:, cols],
                start=True,
                stop=True,
            )

        regroup_halves(nope[0], regroup, FIRST, SECOND)
        quantise(nc, rot[0], WHOLE)
        nc.scalar.copy(out=lat_grouped[:], in_=latT_ps[:].rearrange("p j m -> p m j"))
        nc.scalar.copy(out=tables[:, 1, 0:HALF_ROT], in_=sin_sb[:, HALF_ROT:ROT])
        nc.scalar.mul(tables[:, 1, HALF_ROT:ROT], sin_sb[:, 0:HALF_ROT], -1.0)
        regroup_halves(rot[1], regroup, slice(0, 5 * UNIT // 8), slice(5 * UNIT // 8, UNIT))
        nc.vector.quantize_mx(
            out=lat_codes[:].bitcast(FP8X4),
            scales=lat_scales[:],
            in_=lat_grouped[:].rearrange("p m j -> p (m j)"),
        )
        quantise(nc, nope[0], WHOLE)
        regroup(nc.scalar.copy, nope[1], FIRST)
        quantise(nc, rot[1], WHOLE)

        def product(name, weight, cols=WHOLE):
            acc = psum.tile([P, UNIT], F32, name=name)
            up_product(acc[:, 0 : cols.stop - cols.start], weight, cols)
            return acc

        rot_ps = [product("rot_ps0", rot[0])]
        nope0_ps = product("nope0_ps", nope[0])
        rot_ps.append(product("rot_ps1", rot[1]))

        out_sb = keep.tile([P, HEADS, HEAD], F32)
        products = keep.tile([P, 2, HEADS, ROT], F32)

        def rotate(first_head, heads):
            c, at = divmod(first_head, UNIT_HEADS)
            span = slice(first_head, first_head + heads)
            u = rot_ps[c][:].rearrange("p (h d) -> p h d", d=ROT)[:, at : at + heads, :]
            nc.vector.tensor_tensor(
                out=products[:, :, span, :],
                in0=u.unsqueeze(1).to_broadcast([P, 2, heads, ROT]),
                in1=tables[:].unsqueeze(2).to_broadcast([P, 2, heads, ROT]),
                op=MULT,
            )

        def add_halves(first_head, heads):
            span = slice(first_head, first_head + heads)
            halves = lambda ap: ap.rearrange("p h (s i) -> p h s i", s=2)
            nc.vector.tensor_tensor(
                out=halves(out_sb[:, span, 0:ROT]),
                in0=halves(products[:, 0, span, :]),
                in1=halves(products[:, 1, span, :])[:, :, ::-1, :],
                op=ADD,
            )

        def evacuate_nope(acc, first_head, heads):
            nc.scalar.copy(
                out=out_sb[:, first_head : first_head + heads, ROT:HEAD],
                in_=acc[:, 0 : heads * NOPE].rearrange("p (h d) -> p h d", d=NOPE),
            )

        def store(first_head, heads):
            span = slice(first_head, first_head + heads)
            for b in range(BATCH):
                nc.sync.dma_start(
                    out=out[b, span].rearrange("h t d -> t h d"),
                    in_=out_sb[b:P:BATCH, span, :],
                )

        first, second, third, last = range(0, HEADS, PIECE_HEADS)

        def halves_of(first_head):
            return (first_head, first_head + PIECE_HEADS // 2)

        for head in halves_of(first):
            rotate(head, PIECE_HEADS // 2)
        evacuate_nope(nope0_ps, first, UNIT_HEADS)
        for head in halves_of(first):
            add_halves(head, PIECE_HEADS // 2)
        store(first, PIECE_HEADS)
        rotate(second, PIECE_HEADS)
        quantise(nc, nope[1], FIRST)
        third_ps = product("third_ps", nope[1], FIRST)
        add_halves(second, PIECE_HEADS)
        store(second, PIECE_HEADS)
        regroup(nc.scalar.copy, nope[1], SECOND)
        rotate(third, PIECE_HEADS)
        quantise(nc, nope[1], SECOND)
        last_ps = product("last_ps", nope[1], SECOND)
        evacuate_nope(third_ps, third, PIECE_HEADS)
        add_halves(third, PIECE_HEADS)
        store(third, PIECE_HEADS)
        evacuate_nope(last_ps, last, PIECE_HEADS)
        for head in halves_of(last):
            rotate(head, PIECE_HEADS // 2)
        for head in halves_of(last):
            add_halves(head, PIECE_HEADS // 2)
            store(head, PIECE_HEADS // 2)
